import numpy as np
import ml_dtypes


BF16 = ml_dtypes.bfloat16


def bf(x):
    return np.asarray(x, np.float32).astype(BF16)


def f64(x):
    return np.asarray(x).astype(np.float64)


E2M1 = np.array([0.0, 0.5, 1.0, 1.5, 2.0, 3.0, 4.0, 6.0, -0.0, -0.5, -1.0, -1.5, -2.0, -3.0, -4.0, -6.0])


def pack_weight(w, fmt):
    k, n = w.shape
    w = f64(bf(w)).reshape(k // 32, 32, n)
    amax = np.abs(w).max(1)
    if fmt == "e4m3":
        byte = np.frexp(amax)[1] - 1 + 127 - 7
    else:
        mant, ex = np.frexp(amax / 6.0)
        byte = np.where(mant > 0.5, ex, ex - 1) + 127
    byte = np.clip(np.where(amax > 0, byte, 1), 1, 254)
    scaled = (w * np.exp2(127.0 - byte)[:, None, :]).reshape(k, n).astype(np.float32)
    by_word = np.ascontiguousarray(scaled.reshape(k // 512, 128, 4, n).transpose(0, 1, 3, 2))
    if fmt == "e4m3":
        words = by_word.astype(ml_dtypes.float8_e4m3fn).view(np.uint8)
    else:
        c = by_word.astype(ml_dtypes.float4_e2m1fn).view(np.uint8) & 0xF
        words = c[..., 0::2] | (c[..., 1::2] << 4)
    return np.ascontiguousarray(words), np.ascontiguousarray(byte.astype(np.uint8).reshape(k // 512, 16, n))


def unpack_weight(words, scales, fmt):
    g, p, n, _ = words.shape
    if fmt == "e4m3":
        vals = np.ascontiguousarray(words).view(ml_dtypes.float8_e4m3fn).astype(np.float64)
    else:
        nib = np.empty((g, p, n, 4), np.uint8)
        nib[..., 0::2] = words & 0xF
        nib[..., 1::2] = words >> 4
        vals = E2M1[nib]
    vals = vals * np.repeat(np.exp2(scales.astype(np.float64) - 127.0), 8, axis=1)[..., None]
    return vals.transpose(0, 1, 3, 2).reshape(g * 512, n)

def pack4(w):
    words, scales = pack_weight(w, "e2m1")
    return words.reshape(words.shape[0], 128, -1), scales


def unpack4(words, scales):
    return unpack_weight(words.reshape(words.shape[0], 128, -1, 2), scales, "e2m1")


def kspread(k):
    return np.exp2(np.repeat(np.random.randint(-6, 7, k // 32), 32).astype(np.float64))


B, S, D = 5, 512, 2048
ROPE_BASE = 10000.0


def rope_tables():
    inv_freq = 1.0 / ROPE_BASE ** (np.arange(0, D, 2) / D)
    freqs = np.outer(np.arange(S), inv_freq)
    emb = np.concatenate([freqs, freqs], axis=-1)
    return np.cos(emb), np.sin(emb)


def rotate_half(u):
    u1, u2 = np.split(u, 2, axis=-1)
    return np.concatenate([-u2, u1], axis=-1)


def setup_inputs():
    s = kspread(D)
    c, sn = rope_tables()
    w = 1.0 / np.sqrt(D)
    x = np.random.standard_normal((B, S, D)) * s
    wq = np.random.standard_normal((D, D)) * w / s[None, :]
    wk = np.random.standard_normal((D, D)) * w / s[None, :]
    x_words, x_scales = pack4(np.ascontiguousarray(x.reshape(B * S, D).T))
    wq_words, wq_scales = pack4(np.ascontiguousarray(wq.T))
    wk_words, wk_scales = pack4(np.ascontiguousarray(wk.T))
    return {"x_words": x_words,
            "x_scales": x_scales,
            "cos": bf(c),
            "sin": bf(sn),
            "Wq_words": wq_words,
            "Wq_scales": wq_scales,
            "Wk_words": wk_words,
            "Wk_scales": wk_scales}


def reference(x_words, x_scales, cos, sin, Wq_words, Wq_scales, Wk_words, Wk_scales):
    xq = unpack4(x_words, x_scales).T.reshape(B, S, D)
    q = xq @ unpack4(Wq_words, Wq_scales)
    k = xq @ unpack4(Wk_words, Wk_scales)
    c, sn = f64(cos), f64(sin)
    q_rot = q * c + rotate_half(q) * sn
    k_rot = k * c + rotate_half(k) * sn
    return q_rot, k_rot

@@ -1,0 +1,211 @@
+from contextlib import ExitStack
+
+import concourse.mybir as mybir
+
+F32 = mybir.dt.float32
+BF16 = mybir.dt.bfloat16
+U8 = mybir.dt.uint8
+I32 = mybir.dt.int32
+FP4X4 = mybir.dt.float4_e2m1fn_x4
+MULT = mybir.AluOpType.mult
+ADD = mybir.AluOpType.add
+COPY = mybir.ActivationFunctionType.Copy
+
+BATCH, SEQ, DIM = 5, 512, 2048
+P = 128
+PASSES = DIM // 512
+BANK = 512
+HALF = DIM // 2
+SEQ_TILES = SEQ // P
+
+FLOPS = 2 * BATCH * SEQ * DIM * 2 * DIM
+
+GROUP_SIZES = [1, 1] + [2] * 37 + [1] * 4
+VECTOR_ADDS = 4
+
+
+def tile_attention_pa_kernel(
+    tc, x_words, x_scales, cos, sin, Wq_words, Wq_scales, Wk_words, Wk_scales, out_0, out_1
+):
+    nc = tc.nc
+    w_words = (Wq_words, Wk_words)
+    outs = (out_0, out_1)
+
+    with ExitStack() as ctx:
+        keep = ctx.enter_context(tc.tile_pool(name="keep", bufs=1))
+        prod = ctx.enter_context(tc.tile_pool(name="prod", bufs=4))
+        tail = ctx.enter_context(tc.tile_pool(name="tail", bufs=VECTOR_ADDS))
+        res = ctx.enter_context(tc.tile_pool(name="res", bufs=3))
+        psum = ctx.enter_context(tc.psum_pool(name="psum", bufs=8))
+        ctx.enter_context(tc.manual_schedule())
+
+        def load_codes(dst, words, first_byte, nbytes):
+            nc.sync.dma_start(
+                out=dst[:].bitcast(I32),
+                in_=words[:, :, first_byte : first_byte + nbytes].rearrange("g p n -> p g n").bitcast(I32),
+            )
+
+        def load_scales(dst, scales, first_col, ncols):
+            for q in range(4):
+                nc.sync.dma_start(
+                    out=dst[32 * q : 32 * q + 4, :, :].bitcast(I32),
+                    in_=scales[:, 4 * q : 4 * q + 4, first_col : first_col + ncols]
+                    .rearrange("g r n -> r g n")
+                    .bitcast(I32),
+                )
+
+        def zero(dst):
+            nc.vector.memset(dst[:].bitcast(I32), 0)
+
+        xc00 = keep.tile([P, PASSES, 2 * P], U8, name="xc00", align_bytes=64)
+        xcr0 = keep.tile([P, PASSES, 2 * (SEQ - P)], U8, name="xcr0", align_bytes=64)
+        xb = {}
+        for b in range(1, BATCH):
+            xb[b] = keep.tile([P, PASSES, 2 * SEQ], U8, name="xb%d" % b, align_bytes=64)
+        xs = {}
+        for b in range(BATCH):
+            xs[b] = keep.tile([P, PASSES, SEQ], U8, name="xs%d" % b, align_bytes=64)
+        wc = {}
+        for p in range(2):
+            for blk in range(4):
+                wc[(p, blk)] = keep.tile([P, PASSES, 2 * BANK], U8, name="wc%d_%d" % (p, blk), align_bytes=64)
+        wsq = {}
+        for blk in range(4):
+            wsq[blk] = keep.tile([P, PASSES, BANK], U8, name="wsq%d" % blk, align_bytes=64)
+        wsk = keep.tile([P, PASSES, DIM], U8, name="wsk", align_bytes=64)
+        tab = {}
+        for st in range(SEQ_TILES):
+            for side in range(2):
+                for h in range(2):
+                    tab[(st, side, h)] = keep.tile([P, 2, BANK], BF16, name="tab%d_%d_%d" % (st, side, h))
+        dummy = keep.tile([P, 1], F32, name="dummy")
+
+        def x_codes(st, b, g):
+            if b > 0:
+                return xb[b][:, g, 2 * P * st : 2 * P * (st + 1)]
+            if st == 0:
+                return xc00[:, g, :]
+            return xcr0[:, g, 2 * P * (st - 1) : 2 * P * st]
+
+        def load_x(b):
+            load_scales(xs[b], x_scales, SEQ * b, SEQ)
+            load_codes(xb[b], x_words, 2 * SEQ * b, 2 * SEQ)
+
+        def load_w(p, blk):
+            load_codes(wc[(p, blk)], w_words[p], 2 * BANK * blk, 2 * BANK)
+
+        def load_tab(queue, st, h):
+            rows = slice(P * st, P * (st + 1))
+            ca = slice(BANK * h, BANK * (h + 1))
+            cb = slice(HALF + BANK * h, HALF + BANK * (h + 1))
+            queue.dma_start(out=tab[(st, 0, h)][:, 0, :], in_=cos[rows, ca])
+            queue.dma_start(out=tab[(st, 0, h)][:, 1, :], in_=sin[rows, cb])
+            queue.dma_start(out=tab[(st, 1, h)][:, 0, :], in_=sin[rows, ca])
+            queue.dma_start(out=tab[(st, 1, h)][:, 1, :], in_=cos[rows, cb])
+            nc.scalar.activation(out=tab[(st, 1, h)][:, 0, :], in_=tab[(st, 1, h)][:, 0, :], func=COPY, scale=-1.0)
+
+        nc.gpsimd.memset(dummy[:], 0.0)
+        nc.scalar.activation(out=dummy[:], in_=dummy[:], func=COPY, scale=-1.0)
+        zero(wsq[0])
+        zero(xs[0])
+        zero(wsq[2])
+        for b in range(1, BATCH):
+            zero(xs[b])
+        zero(wsq[1])
+        zero(wsq[3])
+        zero(wsk)
+
+        load_tab(nc.gpsimd, 0, 0)
+
+        load_codes(xc00, x_words, 0, 2 * P)
+        load_w(0, 0)
+        load_scales(wsq[0], Wq_scales, 0, BANK)
+        load_scales(xs[0], x_scales, 0, SEQ)
+        load_w(0, 2)
+        load_scales(wsq[2], Wq_scales, 2 * BANK, BANK)
+        load_codes(xcr0, x_words, 2 * P, 2 * (SEQ - P))
+        for st in range(1, SEQ_TILES):
+            load_tab(nc.sync, st, 0)
+        load_x(1)
+
+        def load_later(u):
+            if u in (0, 2, 4):
+                load_x(2 + u // 2)
+            if u == 6:
+                load_scales(wsq[1], Wq_scales, BANK, BANK)
+                load_w(0, 1)
+                load_scales(wsq[3], Wq_scales, 3 * BANK, BANK)
+                load_w(0, 3)
+            if u in (8, 9, 10, 11):
+                load_tab(nc.sync, u - 8, 1)
+            if u == 14:
+                load_scales(wsk, Wk_scales, 0, DIM)
+                load_w(1, 0)
+                load_w(1, 2)
+            if u == 16:
+                load_w(1, 1)
+                load_w(1, 3)
+
+        def w_scale(p, blk, g):
+            if p == 0:
+                return wsq[blk][:, g, :]
+            return wsk[:, g, BANK * blk : BANK * (blk + 1)]
+
+        def out_view(unit):
+            st, p, h, b = unit
+            return outs[p][b, P * st : P * (st + 1), :].rearrange("s (w hh n) -> s w hh n", w=2, hh=2)[:, :, h, :]
+
+        def add_on_vector(unit, t):
+            o = res.tile([P, 2, BANK], F32, name="o")
+            dst = out_view(unit)
+            for w, queue in ((0, nc.sync), (1, nc.scalar)):
+                cols = slice(BANK * w, BANK * (w + 1))
+                nc.vector.tensor_tensor(out=o[:, w, :], in0=t[:, 0, cols], in1=t[:, 1, cols], op=ADD)
+                queue.dma_start(out=dst[:, w, :], in_=o[:, w, :])
+
+        units = [
+            (st, p, h, b) for p in range(2) for h in range(2) for b in range(BATCH) for st in range(SEQ_TILES)
+        ]
+        late = []
+        first = 0
+        for n in GROUP_SIZES:
+            group = units[first : first + n]
+            on_vector = first + n > len(units) - VECTOR_ADDS
+            if on_vector:
+                t = tail.tile([P, 2, 2 * BANK], F32, name="tv")
+            else:
+                t = prod.tile([P, 2, n * 2 * BANK], F32, name="t")
+            for i, unit in enumerate(group):
+                st, p, h, b = unit
+                for side in range(2):
+                    blk = h + 2 * side
+                    acc = psum.tile([P, 1, BANK], F32, name="acc")
+                    for g in range(PASSES):
+                        nc.tensor.matmul_mx(
+                            out=acc[:, 0, :],
+                            lhsT=x_codes(st, b, g).bitcast(FP4X4),
+                            lhsT_scale=xs[b][:, g, P * st : P * (st + 1)],
+                            rhs=wc[(p, blk)][:, g, :].bitcast(FP4X4),
+                            rhs_scale=w_scale(p, blk, g),
+                            start=(g == 0),
+                            stop=(g == PASSES - 1),
+                        )
+                    nc.vector.tensor_tensor(
+                        out=t[:, side, 2 * BANK * i : 2 * BANK * (i + 1)].rearrange("p (w n) -> p w n", w=2),
+                        in0=acc[:].to_broadcast([P, 2, BANK]),
+                        in1=tab[(st, side, h)][:],
+                        op=MULT,
+                    )
+            if on_vector:
+                late.append((group[0], t))
+            else:
+                o = res.tile([P, n, 2, BANK], F32, name="o")
+                nc.gpsimd.tensor_tensor(
+                    out=o[:].rearrange("p i w n -> p (i w n)"), in0=t[:, 0, :], in1=t[:, 1, :], op=ADD
+                )
+                for i, unit in enumerate(group):
+                    nc.sync.dma_start(out=out_view(unit), in_=o[:, i, :, :])
+                    load_later(first + i)
+            first += n
+        for args in late:
+            add_on_vector(args[0], args[1])

@@ -21,7 +21,7 @@ SEQ_TILES = SEQ // P
 FLOPS = 2 * BATCH * SEQ * DIM * 2 * DIM
 
 GROUP_SIZES = [1, 1] + [2] * 37 + [1] * 4
-VECTOR_ADDS = 4
+VECTOR_ADDS = 1
 
 
 def tile_attention_pa_kernel(
@@ -33,7 +33,7 @@ def tile_attention_pa_kernel(
 
     with ExitStack() as ctx:
         keep = ctx.enter_context(tc.tile_pool(name="keep", bufs=1))
-        prod = ctx.enter_context(tc.tile_pool(name="prod", bufs=4))
+        prod = ctx.enter_context(tc.tile_pool(name="prod", bufs=5))
         tail = ctx.enter_context(tc.tile_pool(name="tail", bufs=VECTOR_ADDS))
         res = ctx.enter_context(tc.tile_pool(name="res", bufs=3))
         psum = ctx.enter_context(tc.psum_pool(name="psum", bufs=8))

@@ -21,7 +21,7 @@ SEQ_TILES = SEQ // P
 FLOPS = 2 * BATCH * SEQ * DIM * 2 * DIM
 
 GROUP_SIZES = [1, 1] + [2] * 37 + [1] * 4
-VECTOR_ADDS = 1
+VECTOR_ADDS = 4
 
 
 def tile_attention_pa_kernel(
@@ -33,7 +33,7 @@ def tile_attention_pa_kernel(
 
     with ExitStack() as ctx:
         keep = ctx.enter_context(tc.tile_pool(name="keep", bufs=1))
-        prod = ctx.enter_context(tc.tile_pool(name="prod", bufs=5))
+        prod = ctx.enter_context(tc.tile_pool(name="prod", bufs=4))
         tail = ctx.enter_context(tc.tile_pool(name="tail", bufs=VECTOR_ADDS))
         res = ctx.enter_context(tc.tile_pool(name="res", bufs=3))
         psum = ctx.enter_context(tc.psum_pool(name="psum", bufs=8))
@@ -177,9 +177,11 @@ def tile_attention_pa_kernel(
                 t = prod.tile([P, 2, n * 2 * BANK], F32, name="t")
             for i, unit in enumerate(group):
                 st, p, h, b = unit
+                accs = []
                 for side in range(2):
                     blk = h + 2 * side
                     acc = psum.tile([P, 1, BANK], F32, name="acc")
+                    accs.append(acc)
                     for g in range(PASSES):
                         nc.tensor.matmul_mx(
                             out=acc[:, 0, :],
@@ -190,9 +192,11 @@ def tile_attention_pa_kernel(
                             start=(g == 0),
                             stop=(g == PASSES - 1),
                         )
+                natural = first + i < 2 or first + i == len(units) - 1
+                for side in (0, 1) if natural else (1, 0):
                     nc.vector.tensor_tensor(
                         out=t[:, side, 2 * BANK * i : 2 * BANK * (i + 1)].rearrange("p (w n) -> p w n", w=2),
-                        in0=acc[:].to_broadcast([P, 2, BANK]),
+                        in0=accs[side][:].to_broadcast([P, 2, BANK]),
                         in1=tab[(st, side, h)][:],
                         op=MULT,
                     )

@@ -20,8 +20,8 @@ SEQ_TILES = SEQ // P
 
 FLOPS = 2 * BATCH * SEQ * DIM * 2 * DIM
 
-GROUP_SIZES = [1, 1] + [2] * 37 + [1] * 4
-VECTOR_ADDS = 4
+GROUP_SIZES = [1, 1] + [2] * 36 + [1] * 6
+VECTOR_ADDS = 5
 
 
 def tile_attention_pa_kernel(
@@ -33,9 +33,8 @@ def tile_attention_pa_kernel(
 
     with ExitStack() as ctx:
         keep = ctx.enter_context(tc.tile_pool(name="keep", bufs=1))
-        prod = ctx.enter_context(tc.tile_pool(name="prod", bufs=4))
+        prod = ctx.enter_context(tc.tile_pool(name="prod", bufs=5))
         tail = ctx.enter_context(tc.tile_pool(name="tail", bufs=VECTOR_ADDS))
-        res = ctx.enter_context(tc.tile_pool(name="res", bufs=3))
         psum = ctx.enter_context(tc.psum_pool(name="psum", bufs=8))
         ctx.enter_context(tc.manual_schedule())
 
@@ -156,12 +155,11 @@ def tile_attention_pa_kernel(
             return outs[p][b, P * st : P * (st + 1), :].rearrange("s (w hh n) -> s w hh n", w=2, hh=2)[:, :, h, :]
 
         def add_on_vector(unit, t):
-            o = res.tile([P, 2, BANK], F32, name="o")
             dst = out_view(unit)
             for w, queue in ((0, nc.sync), (1, nc.scalar)):
                 cols = slice(BANK * w, BANK * (w + 1))
-                nc.vector.tensor_tensor(out=o[:, w, :], in0=t[:, 0, cols], in1=t[:, 1, cols], op=ADD)
-                queue.dma_start(out=dst[:, w, :], in_=o[:, w, :])
+                nc.vector.tensor_tensor(out=t[:, 0, cols], in0=t[:, 0, cols], in1=t[:, 1, cols], op=ADD)
+                queue.dma_start(out=dst[:, w, :], in_=t[:, 0, cols])
 
         units = [
             (st, p, h, b) for p in range(2) for h in range(2) for b in range(BATCH) for st in range(SEQ_TILES)
@@ -177,11 +175,9 @@ def tile_attention_pa_kernel(
                 t = prod.tile([P, 2, n * 2 * BANK], F32, name="t")
             for i, unit in enumerate(group):
                 st, p, h, b = unit
-                accs = []
                 for side in range(2):
                     blk = h + 2 * side
                     acc = psum.tile([P, 1, BANK], F32, name="acc")
-                    accs.append(acc)
                     for g in range(PASSES):
                         nc.tensor.matmul_mx(
                             out=acc[:, 0, :],
@@ -192,23 +188,21 @@ def tile_attention_pa_kernel(
                             start=(g == 0),
                             stop=(g == PASSES - 1),
                         )
-                natural = first + i < 2 or first + i == len(units) - 1
-                for side in (0, 1) if natural else (1, 0):
                     nc.vector.tensor_tensor(
                         out=t[:, side, 2 * BANK * i : 2 * BANK * (i + 1)].rearrange("p (w n) -> p w n", w=2),
-                        in0=accs[side][:].to_broadcast([P, 2, BANK]),
+                        in0=acc[:].to_broadcast([P, 2, BANK]),
                         in1=tab[(st, side, h)][:],
                         op=MULT,
                     )
             if on_vector:
                 late.append((group[0], t))
             else:
-                o = res.tile([P, n, 2, BANK], F32, name="o")
-                nc.gpsimd.tensor_tensor(
-                    out=o[:].rearrange("p i w n -> p (i w n)"), in0=t[:, 0, :], in1=t[:, 1, :], op=ADD
-                )
+                nc.gpsimd.tensor_tensor(out=t[:, 0, :], in0=t[:, 0, :], in1=t[:, 1, :], op=ADD)
                 for i, unit in enumerate(group):
-                    nc.sync.dma_start(out=out_view(unit), in_=o[:, i, :, :])
+                    nc.sync.dma_start(
+                        out=out_view(unit),
+                        in_=t[:, 0, 2 * BANK * i : 2 * BANK * (i + 1)].rearrange("p (w n) -> p w n", w=2),
+                    )
                     load_later(first + i)
             first += n
         for args in late:

@@ -154,7 +154,11 @@ def tile_attention_pa_kernel(
             st, p, h, b = unit
             return outs[p][b, P * st : P * (st + 1), :].rearrange("s (w hh n) -> s w hh n", w=2, hh=2)[:, :, h, :]
 
-        def add_on_vector(unit, t):
+        def add_on_vector(unit, t, queue):
+            nc.vector.tensor_tensor(out=t[:, 0, :], in0=t[:, 0, :], in1=t[:, 1, :], op=ADD)
+            queue.dma_start(out=out_view(unit), in_=t[:, 0, :].rearrange("p (w n) -> p w n", w=2))
+
+        def add_last_on_vector(unit, t):
             dst = out_view(unit)
             for w, queue in ((0, nc.sync), (1, nc.scalar)):
                 cols = slice(BANK * w, BANK * (w + 1))
@@ -175,9 +179,11 @@ def tile_attention_pa_kernel(
                 t = prod.tile([P, 2, n * 2 * BANK], F32, name="t")
             for i, unit in enumerate(group):
                 st, p, h, b = unit
+                accs = []
                 for side in range(2):
                     blk = h + 2 * side
                     acc = psum.tile([P, 1, BANK], F32, name="acc")
+                    accs.append(acc)
                     for g in range(PASSES):
                         nc.tensor.matmul_mx(
                             out=acc[:, 0, :],
@@ -188,9 +194,11 @@ def tile_attention_pa_kernel(
                             start=(g == 0),
                             stop=(g == PASSES - 1),
                         )
+                natural = first + i < 2 or first + i == len(units) - 1
+                for side in (0, 1) if natural else (1, 0):
                     nc.vector.tensor_tensor(
                         out=t[:, side, 2 * BANK * i : 2 * BANK * (i + 1)].rearrange("p (w n) -> p w n", w=2),
-                        in0=acc[:].to_broadcast([P, 2, BANK]),
+                        in0=accs[side][:].to_broadcast([P, 2, BANK]),
                         in1=tab[(st, side, h)][:],
                         op=MULT,
                     )
@@ -205,5 +213,6 @@ def tile_attention_pa_kernel(
                     )
                     load_later(first + i)
             first += n
-        for args in late:
-            add_on_vector(args[0], args[1])
+        for j, args in enumerate(late[:-1]):
+            add_on_vector(args[0], args[1], (nc.sync, nc.scalar)[j % 2])
+        add_last_on_vector(late[-1][0], late[-1][1])

from contextlib import ExitStack

import concourse.mybir as mybir

F32 = mybir.dt.float32
BF16 = mybir.dt.bfloat16
U8 = mybir.dt.uint8
I32 = mybir.dt.int32
FP4X4 = mybir.dt.float4_e2m1fn_x4
MULT = mybir.AluOpType.mult
ADD = mybir.AluOpType.add
COPY = mybir.ActivationFunctionType.Copy

BATCH, SEQ, DIM = 5, 512, 2048
P = 128
PASSES = DIM // 512
BANK = 512
HALF = DIM // 2
SEQ_TILES = SEQ // P

FLOPS = 2 * BATCH * SEQ * DIM * 2 * DIM

GROUP_SIZES = [1, 1] + [2] * 36 + [1] * 6
VECTOR_ADDS = 5


def tile_attention_pa_kernel(
    tc, x_words, x_scales, cos, sin, Wq_words, Wq_scales, Wk_words, Wk_scales, out_0, out_1
):
    nc = tc.nc
    w_words = (Wq_words, Wk_words)
    outs = (out_0, out_1)

    with ExitStack() as ctx:
        keep = ctx.enter_context(tc.tile_pool(name="keep", bufs=1))
        prod = ctx.enter_context(tc.tile_pool(name="prod", bufs=5))
        tail = ctx.enter_context(tc.tile_pool(name="tail", bufs=VECTOR_ADDS))
        psum = ctx.enter_context(tc.psum_pool(name="psum", bufs=8))
        ctx.enter_context(tc.manual_schedule())

        def load_codes(dst, words, first_byte, nbytes):
            nc.sync.dma_start(
                out=dst[:].bitcast(I32),
                in_=words[:, :, first_byte : first_byte + nbytes].rearrange("g p n -> p g n").bitcast(I32),
            )

        def load_scales(dst, scales, first_col, ncols):
            for q in range(4):
                nc.sync.dma_start(
                    out=dst[32 * q : 32 * q + 4, :, :].bitcast(I32),
                    in_=scales[:, 4 * q : 4 * q + 4, first_col : first_col + ncols]
                    .rearrange("g r n -> r g n")
                    .bitcast(I32),
                )

        def zero(dst):
            nc.vector.memset(dst[:].bitcast(I32), 0)

        xc00 = keep.tile([P, PASSES, 2 * P], U8, name="xc00", align_bytes=64)
        xcr0 = keep.tile([P, PASSES, 2 * (SEQ - P)], U8, name="xcr0", align_bytes=64)
        xb = {}
        for b in range(1, BATCH):
            xb[b] = keep.tile([P, PASSES, 2 * SEQ], U8, name="xb%d" % b, align_bytes=64)
        xs = {}
        for b in range(BATCH):
            xs[b] = keep.tile([P, PASSES, SEQ], U8, name="xs%d" % b, align_bytes=64)
        wc = {}
        for p in range(2):
            for blk in range(4):
                wc[(p, blk)] = keep.tile([P, PASSES, 2 * BANK], U8, name="wc%d_%d" % (p, blk), align_bytes=64)
        wsq = {}
        for blk in range(4):
            wsq[blk] = keep.tile([P, PASSES, BANK], U8, name="wsq%d" % blk, align_bytes=64)
        wsk = keep.tile([P, PASSES, DIM], U8, name="wsk", align_bytes=64)
        tab = {}
        for st in range(SEQ_TILES):
            for side in range(2):
                for h in range(2):
                    tab[(st, side, h)] = keep.tile([P, 2, BANK], BF16, name="tab%d_%d_%d" % (st, side, h))
        dummy = keep.tile([P, 1], F32, name="dummy")

        def x_codes(st, b, g):
            if b > 0:
                return xb[b][:, g, 2 * P * st : 2 * P * (st + 1)]
            if st == 0:
                return xc00[:, g, :]
            return xcr0[:, g, 2 * P * (st - 1) : 2 * P * st]

        def load_x(b):
            load_scales(xs[b], x_scales, SEQ * b, SEQ)
            load_codes(xb[b], x_words, 2 * SEQ * b, 2 * SEQ)

        def load_w(p, blk):
            load_codes(wc[(p, blk)], w_words[p], 2 * BANK * blk, 2 * BANK)

        def load_tab(queue, st, h):
            rows = slice(P * st, P * (st + 1))
            ca = slice(BANK * h, BANK * (h + 1))
            cb = slice(HALF + BANK * h, HALF + BANK * (h + 1))
            queue.dma_start(out=tab[(st, 0, h)][:, 0, :], in_=cos[rows, ca])
            queue.dma_start(out=tab[(st, 0, h)][:, 1, :], in_=sin[rows, cb])
            queue.dma_start(out=tab[(st, 1, h)][:, 0, :], in_=sin[rows, ca])
            queue.dma_start(out=tab[(st, 1, h)][:, 1, :], in_=cos[rows, cb])
            nc.scalar.activation(out=tab[(st, 1, h)][:, 0, :], in_=tab[(st, 1, h)][:, 0, :], func=COPY, scale=-1.0)

        nc.gpsimd.memset(dummy[:], 0.0)
        nc.scalar.activation(out=dummy[:], in_=dummy[:], func=COPY, scale=-1.0)
        zero(wsq[0])
        zero(xs[0])
        zero(wsq[2])
        for b in range(1, BATCH):
            zero(xs[b])
        zero(wsq[1])
        zero(wsq[3])
        zero(wsk)

        load_tab(nc.gpsimd, 0, 0)

        load_codes(xc00, x_words, 0, 2 * P)
        load_w(0, 0)
        load_scales(wsq[0], Wq_scales, 0, BANK)
        load_scales(xs[0], x_scales, 0, SEQ)
        load_w(0, 2)
        load_scales(wsq[2], Wq_scales, 2 * BANK, BANK)
        load_codes(xcr0, x_words, 2 * P, 2 * (SEQ - P))
        for st in range(1, SEQ_TILES):
            load_tab(nc.sync, st, 0)
        load_x(1)

        def load_later(u):
            if u in (0, 2, 4):
                load_x(2 + u // 2)
            if u == 6:
                load_scales(wsq[1], Wq_scales, BANK, BANK)
                load_w(0, 1)
                load_scales(wsq[3], Wq_scales, 3 * BANK, BANK)
                load_w(0, 3)
            if u in (8, 9, 10, 11):
                load_tab(nc.sync, u - 8, 1)
            if u == 14:
                load_scales(wsk, Wk_scales, 0, DIM)
                load_w(1, 0)
                load_w(1, 2)
            if u == 16:
                load_w(1, 1)
                load_w(1, 3)

        def w_scale(p, blk, g):
            if p == 0:
                return wsq[blk][:, g, :]
            return wsk[:, g, BANK * blk : BANK * (blk + 1)]

        def out_view(unit):
            st, p, h, b = unit
            return outs[p][b, P * st : P * (st + 1), :].rearrange("s (w hh n) -> s w hh n", w=2, hh=2)[:, :, h, :]

        def add_on_vector(unit, t, queue):
            nc.vector.tensor_tensor(out=t[:, 0, :], in0=t[:, 0, :], in1=t[:, 1, :], op=ADD)
            queue.dma_start(out=out_view(unit), in_=t[:, 0, :].rearrange("p (w n) -> p w n", w=2))

        def add_last_on_vector(unit, t):
            dst = out_view(unit)
            for w, queue in ((0, nc.sync), (1, nc.scalar)):
                cols = slice(BANK * w, BANK * (w + 1))
                nc.vector.tensor_tensor(out=t[:, 0, cols], in0=t[:, 0, cols], in1=t[:, 1, cols], op=ADD)
                queue.dma_start(out=dst[:, w, :], in_=t[:, 0, cols])

        units = [
            (st, p, h, b) for p in range(2) for h in range(2) for b in range(BATCH) for st in range(SEQ_TILES)
        ]
        late = []
        first = 0
        for n in GROUP_SIZES:
            group = units[first : first + n]
            on_vector = first + n > len(units) - VECTOR_ADDS
            if on_vector:
                t = tail.tile([P, 2, 2 * BANK], F32, name="tv")
            else:
                t = prod.tile([P, 2, n * 2 * BANK], F32, name="t")
            for i, unit in enumerate(group):
                st, p, h, b = unit
                accs = []
                for side in range(2):
                    blk = h + 2 * side
                    acc = psum.tile([P, 1, BANK], F32, name="acc")
                    accs.append(acc)
                    for g in range(PASSES):
                        nc.tensor.matmul_mx(
                            out=acc[:, 0, :],
                            lhsT=x_codes(st, b, g).bitcast(FP4X4),
                            lhsT_scale=xs[b][:, g, P * st : P * (st + 1)],
                            rhs=wc[(p, blk)][:, g, :].bitcast(FP4X4),
                            rhs_scale=w_scale(p, blk, g),
                            start=(g == 0),
                            stop=(g == PASSES - 1),
                        )
                natural = first + i < 2 or first + i == len(units) - 1
                for side in (0, 1) if natural else (1, 0):
                    nc.vector.tensor_tensor(
                        out=t[:, side, 2 * BANK * i : 2 * BANK * (i + 1)].rearrange("p (w n) -> p w n", w=2),
                        in0=accs[side][:].to_broadcast([P, 2, BANK]),
                        in1=tab[(st, side, h)][:],
                        op=MULT,
                    )
            if on_vector:
                late.append((group[0], t))
            else:
                nc.gpsimd.tensor_tensor(out=t[:, 0, :], in0=t[:, 0, :], in1=t[:, 1, :], op=ADD)
                for i, unit in enumerate(group):
                    nc.sync.dma_start(
                        out=out_view(unit),
                        in_=t[:, 0, 2 * BANK * i : 2 * BANK * (i + 1)].rearrange("p (w n) -> p w n", w=2),
                    )
                    load_later(first + i)
            first += n
        for j, args in enumerate(late[:-1]):
            add_on_vector(args[0], args[1], (nc.sync, nc.scalar)[j % 2])
        add_last_on_vector(late[-1][0], late[-1][1])
